import numpy as np
import ml_dtypes

BF16 = ml_dtypes.bfloat16


def bf(x):
    return np.asarray(x, np.float32).astype(BF16)


def f32(x):
    return np.asarray(x, np.float32)


def f64(x):
    return np.asarray(x).astype(np.float64)


def striped(idx):
    return np.tile(idx.reshape(-1, 16).T, (8, 1))


CI, M, S, N = 256, 128, 512, 128
EDGE_P = 0.05
SLOPE = 0.01


def setup_inputs():
    lim = np.sqrt(6.0 / (CI + M))
    up = np.triu((np.random.uniform(size=(N, N)) < EDGE_P).astype(np.float32), 1)
    return {"base": f32(np.random.standard_normal((M, S))), "x": bf(np.random.standard_normal((CI, N))), "w": bf(np.random.uniform(-lim, lim, (CI, M))), "adj": bf(up + up.T), "bias": f32(0.1 * np.random.standard_normal((M, 1))), "offs": striped(np.random.permutation(S)[:N])}


def reference(base, x, w, adj, bias, offs):
    idx = offs[:16].T.reshape(-1)
    a = f64(adj) + np.eye(N)
    dinv = 1.0 / np.sqrt(a.sum(axis=1))
    h = f64(w).T @ f64(x)
    v = ((h * dinv[None, :]) @ a.T) * dinv[None, :] + f64(bias)
    slope = np.where(v > 0.0, 1.0, SLOPE)
    out = f64(base).copy()
    out[:, idx] = v * slope
    return out

@@ -1,0 +1,72 @@
+import concourse.mybir as mybir
+from concourse.masks import make_identity
+
+CI, M, S, N = 256, 128, 512, 128
+P = 128
+SLOPE = 0.01
+FLOPS = 2 * CI * M * N + 2 * N * N * M
+
+BF16, F32, U16 = mybir.dt.bfloat16, mybir.dt.float32, mybir.dt.uint16
+ALU = mybir.AluOpType
+FUNC = mybir.ActivationFunctionType
+
+
+def tile_gcnconv_kernel(tc, base, x, w, adj, bias, offs, out):
+    nc = tc.nc
+    blocks = CI // P
+    with tc.tile_pool(name="held", bufs=1) as held, tc.psum_pool(name="psum", bufs=1) as psum:
+        adj_sb = held.tile([N, N], BF16)
+        nc.sync.dma_start(adj_sb[:], adj)
+        x_sb = held.tile([P, blocks, N], BF16)
+        nc.scalar.dma_start(x_sb[:], x.rearrange("(p c) k -> p c k", c=blocks))
+        w_sb = held.tile([P, blocks, M], BF16)
+        nc.scalar.dma_start(w_sb[:], w.rearrange("(p c) m -> p c m", c=blocks))
+        offsets = held.tile([P, N // 16], U16, name="offsets")
+        nc.sync.dma_start(offsets[:], offs)
+        bias_sb = held.tile([M, 1], F32)
+        nc.scalar.dma_start(bias_sb[:], bias)
+        window = held.tile([M, S], F32)
+        nc.sync.dma_start(window[:], base)
+
+        ident = held.tile([N, N], BF16)
+        make_identity(nc, ident[:])
+        ones = held.tile([N, M], BF16)
+        nc.gpsimd.memset(ones[:], 1.0)
+
+        a_sb = held.tile([N, N], BF16)
+        nc.vector.tensor_tensor(a_sb[:], adj_sb[:], ident[:], ALU.add)
+        deg_col = held.tile([N, 1], F32)
+        nc.vector.reduce_sum(deg_col[:], a_sb[:], axis=mybir.AxisListType.X)
+        deg_rows_ps = psum.tile([M, N], F32)
+        nc.tensor.matmul(deg_rows_ps[:], ones[:], a_sb[:], start=True, stop=True)
+
+        root_col = held.tile([N, 1], F32)
+        nc.scalar.activation(root_col[:], deg_col[:], FUNC.Sqrt)
+        dinv_col = held.tile([N, 1], F32)
+        nc.vector.reciprocal(dinv_col[:], root_col[:])
+
+        hT_ps = psum.tile([N, M], F32)
+        for c in range(blocks):
+            nc.tensor.matmul(
+                hT_ps[:], x_sb[:, c, :], w_sb[:, c, :], start=(c == 0), stop=(c == blocks - 1)
+            )
+        gT = held.tile([N, M], BF16)
+        nc.vector.tensor_scalar_mul(gT[:], hT_ps[:], dinv_col[:, 0:1])
+
+        agg_ps = psum.tile([M, N], F32)
+        nc.tensor.matmul(agg_ps[:], gT[:], a_sb[:], start=True, stop=True)
+
+        root_rows = held.tile([M, N], F32)
+        nc.scalar.activation(root_rows[:], deg_rows_ps[:], FUNC.Sqrt)
+        dinv_rows = held.tile([M, N], F32)
+        nc.vector.reciprocal(dinv_rows[:], root_rows[:])
+
+        scaled = held.tile([M, N], F32)
+        nc.vector.tensor_tensor(scaled[:], agg_ps[:], dinv_rows[:], ALU.mult)
+        v = held.tile([M, N], F32)
+        nc.vector.tensor_scalar_add(v[:], scaled[:], bias_sb[:, 0:1])
+        slope = held.tile([M, N], F32)
+        nc.vector.tensor_scalar(slope[:], v[:], 0.0, SLOPE, ALU.is_gt, ALU.max)
+
+        nc.vector.tensor_tensor(window[:].indirect(offsets[:]), v[:], slope[:], ALU.mult)
+        nc.sync.dma_start(out, window[:])

@@ -40,10 +40,10 @@ def tile_gcnconv_kernel(tc, base, x, w, adj, bias, offs, out):
         deg_rows_ps = psum.tile([M, N], F32)
         nc.tensor.matmul(deg_rows_ps[:], ones[:], a_sb[:], start=True, stop=True)
 
-        root_col = held.tile([N, 1], F32)
-        nc.scalar.activation(root_col[:], deg_col[:], FUNC.Sqrt)
         dinv_col = held.tile([N, 1], F32)
-        nc.vector.reciprocal(dinv_col[:], root_col[:])
+        nc.scalar.activation(dinv_col[:], deg_col[:], FUNC.Abs_reciprocal_sqrt)
+        dinv_rows = held.tile([M, N], F32)
+        nc.scalar.activation(dinv_rows[:], deg_rows_ps[:], FUNC.Abs_reciprocal_sqrt)
 
         hT_ps = psum.tile([N, M], F32)
         for c in range(blocks):
@@ -55,11 +55,6 @@ def tile_gcnconv_kernel(tc, base, x, w, adj, bias, offs, out):
 
         agg_ps = psum.tile([M, N], F32)
         nc.tensor.matmul(agg_ps[:], gT[:], a_sb[:], start=True, stop=True)
-
-        root_rows = held.tile([M, N], F32)
-        nc.scalar.activation(root_rows[:], deg_rows_ps[:], FUNC.Sqrt)
-        dinv_rows = held.tile([M, N], F32)
-        nc.vector.reciprocal(dinv_rows[:], root_rows[:])
 
         scaled = held.tile([M, N], F32)
         nc.vector.tensor_tensor(scaled[:], agg_ps[:], dinv_rows[:], ALU.mult)

@@ -20,7 +20,7 @@ def tile_gcnconv_kernel(tc, base, x, w, adj, bias, offs, out):
         x_sb = held.tile([P, blocks, N], BF16)
         nc.scalar.dma_start(x_sb[:], x.rearrange("(p c) k -> p c k", c=blocks))
         w_sb = held.tile([P, blocks, M], BF16)
-        nc.scalar.dma_start(w_sb[:], w.rearrange("(p c) m -> p c m", c=blocks))
+        nc.sync.dma_start(w_sb[:], w.rearrange("(p c) m -> p c m", c=blocks))
         offsets = held.tile([P, N // 16], U16, name="offsets")
         nc.sync.dma_start(offsets[:], offs)
         bias_sb = held.tile([M, 1], F32)
@@ -33,17 +33,18 @@ def tile_gcnconv_kernel(tc, base, x, w, adj, bias, offs, out):
         ones = held.tile([N, M], BF16)
         nc.gpsimd.memset(ones[:], 1.0)
 
-        a_sb = held.tile([N, N], BF16)
-        nc.vector.tensor_tensor(a_sb[:], adj_sb[:], ident[:], ALU.add)
-        deg_col = held.tile([N, 1], F32)
-        nc.vector.reduce_sum(deg_col[:], a_sb[:], axis=mybir.AxisListType.X)
-        deg_rows_ps = psum.tile([M, N], F32)
-        nc.tensor.matmul(deg_rows_ps[:], ones[:], a_sb[:], start=True, stop=True)
+        nbrs_col = held.tile([N, 1], F32)
+        nc.vector.reduce_sum(nbrs_col[:], adj_sb[:], axis=mybir.AxisListType.X)
+        nbrs_rows_ps = psum.tile([M, N], F32)
+        nc.tensor.matmul(nbrs_rows_ps[:], ones[:], adj_sb[:], start=True, stop=True)
 
         dinv_col = held.tile([N, 1], F32)
-        nc.scalar.activation(dinv_col[:], deg_col[:], FUNC.Abs_reciprocal_sqrt)
+        nc.scalar.activation(dinv_col[:], nbrs_col[:], FUNC.Abs_reciprocal_sqrt, bias=1.0)
         dinv_rows = held.tile([M, N], F32)
-        nc.scalar.activation(dinv_rows[:], deg_rows_ps[:], FUNC.Abs_reciprocal_sqrt)
+        nc.scalar.activation(dinv_rows[:], nbrs_rows_ps[:], FUNC.Abs_reciprocal_sqrt, bias=1.0)
+
+        a_sb = held.tile([N, N], BF16)
+        nc.vector.tensor_tensor(a_sb[:], adj_sb[:], ident[:], ALU.add)
 
         hT_ps = psum.tile([N, M], F32)
         for c in range(blocks):

@@ -65,4 +65,8 @@ def tile_gcnconv_kernel(tc, base, x, w, adj, bias, offs, out):
         nc.vector.tensor_scalar(slope[:], v[:], 0.0, SLOPE, ALU.is_gt, ALU.max)
 
         nc.vector.tensor_tensor(window[:].indirect(offsets[:]), v[:], slope[:], ALU.mult)
-        nc.sync.dma_start(out, window[:])
+        pieces = 4
+        width = S // pieces
+        for i in range(pieces):
+            queue = nc.sync if i % 2 == 0 else nc.scalar
+            queue.dma_start(out[:, i * width : (i + 1) * width], window[:, i * width : (i + 1) * width])

@@ -28,6 +28,9 @@ def tile_gcnconv_kernel(tc, base, x, w, adj, bias, offs, out):
         window = held.tile([M, S], F32)
         nc.sync.dma_start(window[:], base)
 
+        neg_bias = held.tile([M, 1], F32)
+        nc.gpsimd.tensor_scalar_mul(neg_bias[:], bias_sb[:], -1.0)
+
         ident = held.tile([N, N], BF16)
         make_identity(nc, ident[:])
         ones = held.tile([N, M], BF16)
@@ -62,11 +65,7 @@ def tile_gcnconv_kernel(tc, base, x, w, adj, bias, offs, out):
         v = held.tile([M, N], F32)
         nc.vector.tensor_scalar_add(v[:], scaled[:], bias_sb[:, 0:1])
         slope = held.tile([M, N], F32)
-        nc.vector.tensor_scalar(slope[:], v[:], 0.0, SLOPE, ALU.is_gt, ALU.max)
+        nc.vector.tensor_scalar(slope[:], scaled[:], neg_bias[:, 0:1], SLOPE, ALU.is_gt, ALU.max)
 
         nc.vector.tensor_tensor(window[:].indirect(offsets[:]), v[:], slope[:], ALU.mult)
-        pieces = 4
-        width = S // pieces
-        for i in range(pieces):
-            queue = nc.sync if i % 2 == 0 else nc.scalar
-            queue.dma_start(out[:, i * width : (i + 1) * width], window[:, i * width : (i + 1) * width])
+        nc.sync.dma_start(out, window[:])

@@ -43,8 +43,6 @@ def tile_gcnconv_kernel(tc, base, x, w, adj, bias, offs, out):
 
         dinv_col = held.tile([N, 1], F32)
         nc.scalar.activation(dinv_col[:], nbrs_col[:], FUNC.Abs_reciprocal_sqrt, bias=1.0)
-        dinv_rows = held.tile([M, N], F32)
-        nc.scalar.activation(dinv_rows[:], nbrs_rows_ps[:], FUNC.Abs_reciprocal_sqrt, bias=1.0)
 
         a_sb = held.tile([N, N], BF16)
         nc.vector.tensor_tensor(a_sb[:], adj_sb[:], ident[:], ALU.add)
@@ -55,7 +53,10 @@ def tile_gcnconv_kernel(tc, base, x, w, adj, bias, offs, out):
                 hT_ps[:], x_sb[:, c, :], w_sb[:, c, :], start=(c == 0), stop=(c == blocks - 1)
             )
         gT = held.tile([N, M], BF16)
-        nc.vector.tensor_scalar_mul(gT[:], hT_ps[:], dinv_col[:, 0:1])
+        nc.scalar.activation(gT[:], hT_ps[:], FUNC.Copy, scale=dinv_col[:, 0:1])
+
+        dinv_rows = held.tile([M, N], F32)
+        nc.scalar.activation(dinv_rows[:], nbrs_rows_ps[:], FUNC.Abs_reciprocal_sqrt, bias=1.0)
 
         agg_ps = psum.tile([M, N], F32)
         nc.tensor.matmul(agg_ps[:], gT[:], a_sb[:], start=True, stop=True)

@@ -18,13 +18,13 @@ def tile_gcnconv_kernel(tc, base, x, w, adj, bias, offs, out):
         adj_sb = held.tile([N, N], BF16)
         nc.sync.dma_start(adj_sb[:], adj)
         x_sb = held.tile([P, blocks, N], BF16)
-        nc.scalar.dma_start(x_sb[:], x.rearrange("(p c) k -> p c k", c=blocks))
+        nc.sync.dma_start(x_sb[:], x.rearrange("(p c) k -> p c k", c=blocks))
         w_sb = held.tile([P, blocks, M], BF16)
         nc.sync.dma_start(w_sb[:], w.rearrange("(p c) m -> p c m", c=blocks))
         offsets = held.tile([P, N // 16], U16, name="offsets")
         nc.sync.dma_start(offsets[:], offs)
         bias_sb = held.tile([M, 1], F32)
-        nc.scalar.dma_start(bias_sb[:], bias)
+        nc.sync.dma_start(bias_sb[:], bias)
         window = held.tile([M, S], F32)
         nc.sync.dma_start(window[:], base)
 

@@ -19,8 +19,10 @@ def tile_gcnconv_kernel(tc, base, x, w, adj, bias, offs, out):
         nc.sync.dma_start(adj_sb[:], adj)
         x_sb = held.tile([P, blocks, N], BF16)
         nc.sync.dma_start(x_sb[:], x.rearrange("(p c) k -> p c k", c=blocks))
-        w_sb = held.tile([P, blocks, M], BF16)
-        nc.sync.dma_start(w_sb[:], w.rearrange("(p c) m -> p c m", c=blocks))
+        w_view = w.rearrange("(p c) m -> p c m", c=blocks)
+        w_blocks = [held.tile([P, M], BF16, name="w%d" % c) for c in range(blocks)]
+        for c in range(blocks):
+            nc.sync.dma_start(w_blocks[c][:], w_view[:, c, :])
         offsets = held.tile([P, N // 16], U16, name="offsets")
         nc.sync.dma_start(offsets[:], offs)
         bias_sb = held.tile([M, 1], F32)
@@ -50,7 +52,7 @@ def tile_gcnconv_kernel(tc, base, x, w, adj, bias, offs, out):
         hT_ps = psum.tile([N, M], F32)
         for c in range(blocks):
             nc.tensor.matmul(
-                hT_ps[:], x_sb[:, c, :], w_sb[:, c, :], start=(c == 0), stop=(c == blocks - 1)
+                hT_ps[:], x_sb[:, c, :], w_blocks[c][:], start=(c == 0), stop=(c == blocks - 1)
             )
         gT = held.tile([N, M], BF16)
         nc.scalar.activation(gT[:], hT_ps[:], FUNC.Copy, scale=dinv_col[:, 0:1])

@@ -23,12 +23,12 @@ def tile_gcnconv_kernel(tc, base, x, w, adj, bias, offs, out):
         w_blocks = [held.tile([P, M], BF16, name="w%d" % c) for c in range(blocks)]
         for c in range(blocks):
             nc.sync.dma_start(w_blocks[c][:], w_view[:, c, :])
+        window = held.tile([M, S], F32)
+        nc.sync.dma_start(window[:], base)
         offsets = held.tile([P, N // 16], U16, name="offsets")
         nc.sync.dma_start(offsets[:], offs)
         bias_sb = held.tile([M, 1], F32)
         nc.sync.dma_start(bias_sb[:], bias)
-        window = held.tile([M, S], F32)
-        nc.sync.dma_start(window[:], base)
 
         neg_bias = held.tile([M, 1], F32)
         nc.gpsimd.tensor_scalar_mul(neg_bias[:], bias_sb[:], -1.0)

@@ -35,19 +35,36 @@ def tile_gcnconv_kernel(tc, base, x, w, adj, bias, offs, out):
 
         ident = held.tile([N, N], BF16)
         make_identity(nc, ident[:])
-        ones = held.tile([N, M], BF16)
+        ones = held.tile([N, N], BF16)
         nc.gpsimd.memset(ones[:], 1.0)
 
         nbrs_col = held.tile([N, 1], F32)
         nc.vector.reduce_sum(nbrs_col[:], adj_sb[:], axis=mybir.AxisListType.X)
-        nbrs_rows_ps = psum.tile([M, N], F32)
-        nc.tensor.matmul(nbrs_rows_ps[:], ones[:], adj_sb[:], start=True, stop=True)
+        halves = [slice(0, N // 2), slice(N // 2, N)]
+        nbrs_rows_ps = [psum.tile([N, N // 2], F32, name="nbrs%d" % i) for i in range(2)]
+        for i, half in enumerate(halves):
+            nc.tensor.matmul(nbrs_rows_ps[i][:], ones[:], adj_sb[:, half], start=True, stop=True)
 
+        dinv_rows = held.tile([N, N], F32)
+        for i, half in enumerate(halves):
+            nc.scalar.activation(
+                dinv_rows[:, half], nbrs_rows_ps[i][:], FUNC.Abs_reciprocal_sqrt, bias=1.0
+            )
         dinv_col = held.tile([N, 1], F32)
         nc.scalar.activation(dinv_col[:], nbrs_col[:], FUNC.Abs_reciprocal_sqrt, bias=1.0)
 
         a_sb = held.tile([N, N], BF16)
         nc.vector.tensor_tensor(a_sb[:], adj_sb[:], ident[:], ALU.add)
+
+        a_dinv = held.tile([N, N], F32)
+        for half in halves:
+            nc.vector.tensor_tensor(a_dinv[:, half], a_sb[:, half], dinv_rows[:, half], ALU.mult)
+        a_high = a_dinv[:].bitcast(BF16)[:, 1::2]
+        a_low = held.tile([N, N], BF16)
+        for half in halves:
+            nc.vector.tensor_tensor(
+                a_low[:, half], a_dinv[:, half], a_high[:, half], ALU.subtract
+            )
 
         hT_ps = psum.tile([N, M], F32)
         for c in range(blocks):
@@ -57,18 +74,18 @@ def tile_gcnconv_kernel(tc, base, x, w, adj, bias, offs, out):
         gT = held.tile([N, M], BF16)
         nc.scalar.activation(gT[:], hT_ps[:], FUNC.Copy, scale=dinv_col[:, 0:1])
 
-        dinv_rows = held.tile([M, N], F32)
-        nc.scalar.activation(dinv_rows[:], nbrs_rows_ps[:], FUNC.Abs_reciprocal_sqrt, bias=1.0)
+        agg_ps = [psum.tile([M, N // 2], F32, name="agg%d" % i) for i in range(2)]
+        for i, half in enumerate(halves):
+            nc.tensor.matmul(agg_ps[i][:], gT[:], a_high[:, half], start=True, stop=False)
+            nc.tensor.matmul(agg_ps[i][:], gT[:], a_low[:, half], start=False, stop=True)
 
-        agg_ps = psum.tile([M, N], F32)
-        nc.tensor.matmul(agg_ps[:], gT[:], a_sb[:], start=True, stop=True)
-
-        scaled = held.tile([M, N], F32)
-        nc.vector.tensor_tensor(scaled[:], agg_ps[:], dinv_rows[:], ALU.mult)
         v = held.tile([M, N], F32)
-        nc.vector.tensor_scalar_add(v[:], scaled[:], bias_sb[:, 0:1])
         slope = held.tile([M, N], F32)
-        nc.vector.tensor_scalar(slope[:], scaled[:], neg_bias[:, 0:1], SLOPE, ALU.is_gt, ALU.max)
+        for i, half in enumerate(halves):
+            nc.vector.tensor_scalar_add(v[:, half], agg_ps[i][:], bias_sb[:, 0:1])
+            nc.vector.tensor_scalar(
+                slope[:, half], agg_ps[i][:], neg_bias[:, 0:1], SLOPE, ALU.is_gt, ALU.max
+            )
 
         nc.vector.tensor_tensor(window[:].indirect(offsets[:]), v[:], slope[:], ALU.mult)
         nc.sync.dma_start(out, window[:])

@@ -30,13 +30,10 @@ def tile_gcnconv_kernel(tc, base, x, w, adj, bias, offs, out):
         bias_sb = held.tile([M, 1], F32)
         nc.sync.dma_start(bias_sb[:], bias)
 
-        neg_bias = held.tile([M, 1], F32)
-        nc.gpsimd.tensor_scalar_mul(neg_bias[:], bias_sb[:], -1.0)
-
         ident = held.tile([N, N], BF16)
         make_identity(nc, ident[:])
         ones = held.tile([N, N], BF16)
-        nc.gpsimd.memset(ones[:], 1.0)
+        nc.vector.memset(ones[:], 1.0)
 
         nbrs_col = held.tile([N, 1], F32)
         nc.vector.reduce_sum(nbrs_col[:], adj_sb[:], axis=mybir.AxisListType.X)
@@ -73,6 +70,8 @@ def tile_gcnconv_kernel(tc, base, x, w, adj, bias, offs, out):
             )
         gT = held.tile([N, M], BF16)
         nc.scalar.activation(gT[:], hT_ps[:], FUNC.Copy, scale=dinv_col[:, 0:1])
+        neg_bias = held.tile([M, 1], F32)
+        nc.scalar.mul(neg_bias[:], bias_sb[:], -1.0)
 
         agg_ps = [psum.tile([M, N // 2], F32, name="agg%d" % i) for i in range(2)]
         for i, half in enumerate(halves):

@@ -50,12 +50,14 @@ def tile_gcnconv_kernel(tc, base, x, w, adj, bias, offs, out):
         dinv_col = held.tile([N, 1], F32)
         nc.scalar.activation(dinv_col[:], nbrs_col[:], FUNC.Abs_reciprocal_sqrt, bias=1.0)
 
-        a_sb = held.tile([N, N], BF16)
-        nc.vector.tensor_tensor(a_sb[:], adj_sb[:], ident[:], ALU.add)
+        minus_a = held.tile([N, N], BF16)
+        nc.vector.scalar_tensor_tensor(
+            minus_a[:], adj_sb[:], -1.0, ident[:], ALU.mult, ALU.subtract
+        )
 
         a_dinv = held.tile([N, N], F32)
         for half in halves:
-            nc.vector.tensor_tensor(a_dinv[:, half], a_sb[:, half], dinv_rows[:, half], ALU.mult)
+            nc.vector.tensor_tensor(a_dinv[:, half], minus_a[:, half], dinv_rows[:, half], ALU.mult)
         a_high = a_dinv[:].bitcast(BF16)[:, 1::2]
         a_low = held.tile([N, N], BF16)
         for half in halves:
@@ -70,8 +72,6 @@ def tile_gcnconv_kernel(tc, base, x, w, adj, bias, offs, out):
             )
         gT = held.tile([N, M], BF16)
         nc.scalar.activation(gT[:], hT_ps[:], FUNC.Copy, scale=dinv_col[:, 0:1])
-        neg_bias = held.tile([M, 1], F32)
-        nc.scalar.mul(neg_bias[:], bias_sb[:], -1.0)
 
         agg_ps = [psum.tile([M, N // 2], F32, name="agg%d" % i) for i in range(2)]
         for i, half in enumerate(halves):
@@ -81,9 +81,11 @@ def tile_gcnconv_kernel(tc, base, x, w, adj, bias, offs, out):
         v = held.tile([M, N], F32)
         slope = held.tile([M, N], F32)
         for i, half in enumerate(halves):
-            nc.vector.tensor_scalar_add(v[:, half], agg_ps[i][:], bias_sb[:, 0:1])
             nc.vector.tensor_scalar(
-                slope[:, half], agg_ps[i][:], neg_bias[:, 0:1], SLOPE, ALU.is_gt, ALU.max
+                v[:, half], agg_ps[i][:], -1.0, bias_sb[:, 0:1], ALU.mult, ALU.add
+            )
+            nc.vector.tensor_scalar(
+                slope[:, half], agg_ps[i][:], bias_sb[:, 0:1], SLOPE, ALU.is_lt, ALU.max
             )
 
         nc.vector.tensor_tensor(window[:].indirect(offsets[:]), v[:], slope[:], ALU.mult)

@@ -35,8 +35,12 @@ def tile_gcnconv_kernel(tc, base, x, w, adj, bias, offs, out):
         ones = held.tile([N, N], BF16)
         nc.vector.memset(ones[:], 1.0)
 
-        nbrs_col = held.tile([N, 1], F32)
-        nc.vector.reduce_sum(nbrs_col[:], adj_sb[:], axis=mybir.AxisListType.X)
+        minus_a = held.tile([N, N], BF16)
+        minus_deg = held.tile([N, 1], F32)
+        nc.vector.scalar_tensor_tensor(
+            minus_a[:], adj_sb[:], -1.0, ident[:], ALU.mult, ALU.subtract, accum_out=minus_deg[:]
+        )
+
         halves = [slice(0, N // 2), slice(N // 2, N)]
         nbrs_rows_ps = [psum.tile([N, N // 2], F32, name="nbrs%d" % i) for i in range(2)]
         for i, half in enumerate(halves):
@@ -48,12 +52,7 @@ def tile_gcnconv_kernel(tc, base, x, w, adj, bias, offs, out):
                 dinv_rows[:, half], nbrs_rows_ps[i][:], FUNC.Abs_reciprocal_sqrt, bias=1.0
             )
         dinv_col = held.tile([N, 1], F32)
-        nc.scalar.activation(dinv_col[:], nbrs_col[:], FUNC.Abs_reciprocal_sqrt, bias=1.0)
-
-        minus_a = held.tile([N, N], BF16)
-        nc.vector.scalar_tensor_tensor(
-            minus_a[:], adj_sb[:], -1.0, ident[:], ALU.mult, ALU.subtract
-        )
+        nc.scalar.activation(dinv_col[:], minus_deg[:], FUNC.Abs_reciprocal_sqrt)
 
         a_dinv = held.tile([N, N], F32)
         for half in halves:

@@ -72,19 +72,20 @@ def tile_gcnconv_kernel(tc, base, x, w, adj, bias, offs, out):
         gT = held.tile([N, M], BF16)
         nc.scalar.activation(gT[:], hT_ps[:], FUNC.Copy, scale=dinv_col[:, 0:1])
 
-        agg_ps = [psum.tile([M, N // 2], F32, name="agg%d" % i) for i in range(2)]
-        for i, half in enumerate(halves):
-            nc.tensor.matmul(agg_ps[i][:], gT[:], a_high[:, half], start=True, stop=False)
-            nc.tensor.matmul(agg_ps[i][:], gT[:], a_low[:, half], start=False, stop=True)
+        quarters = [slice(q * N // 4, (q + 1) * N // 4) for q in range(4)]
+        agg_ps = [psum.tile([M, N // 4], F32, name="agg%d" % i) for i in range(4)]
+        for i, quarter in enumerate(quarters):
+            nc.tensor.matmul(agg_ps[i][:], gT[:], a_high[:, quarter], start=True, stop=False)
+            nc.tensor.matmul(agg_ps[i][:], gT[:], a_low[:, quarter], start=False, stop=True)
 
         v = held.tile([M, N], F32)
         slope = held.tile([M, N], F32)
-        for i, half in enumerate(halves):
+        for i, quarter in enumerate(quarters):
             nc.vector.tensor_scalar(
-                v[:, half], agg_ps[i][:], -1.0, bias_sb[:, 0:1], ALU.mult, ALU.add
+                v[:, quarter], agg_ps[i][:], -1.0, bias_sb[:, 0:1], ALU.mult, ALU.add
             )
             nc.vector.tensor_scalar(
-                slope[:, half], agg_ps[i][:], bias_sb[:, 0:1], SLOPE, ALU.is_lt, ALU.max
+                slope[:, quarter], agg_ps[i][:], bias_sb[:, 0:1], SLOPE, ALU.is_lt, ALU.max
             )
 
         nc.vector.tensor_tensor(window[:].indirect(offsets[:]), v[:], slope[:], ALU.mult)

import concourse.mybir as mybir
from concourse.masks import make_identity

CI, M, S, N = 256, 128, 512, 128
P = 128
SLOPE = 0.01
FLOPS = 2 * CI * M * N + 2 * N * N * M

BF16, F32, U16 = mybir.dt.bfloat16, mybir.dt.float32, mybir.dt.uint16
ALU = mybir.AluOpType
FUNC = mybir.ActivationFunctionType


def tile_gcnconv_kernel(tc, base, x, w, adj, bias, offs, out):
    nc = tc.nc
    blocks = CI // P
    with tc.tile_pool(name="held", bufs=1) as held, tc.psum_pool(name="psum", bufs=1) as psum:
        adj_sb = held.tile([N, N], BF16)
        nc.sync.dma_start(adj_sb[:], adj)
        x_sb = held.tile([P, blocks, N], BF16)
        nc.sync.dma_start(x_sb[:], x.rearrange("(p c) k -> p c k", c=blocks))
        w_view = w.rearrange("(p c) m -> p c m", c=blocks)
        w_blocks = [held.tile([P, M], BF16, name="w%d" % c) for c in range(blocks)]
        for c in range(blocks):
            nc.sync.dma_start(w_blocks[c][:], w_view[:, c, :])
        window = held.tile([M, S], F32)
        nc.sync.dma_start(window[:], base)
        offsets = held.tile([P, N // 16], U16, name="offsets")
        nc.sync.dma_start(offsets[:], offs)
        bias_sb = held.tile([M, 1], F32)
        nc.sync.dma_start(bias_sb[:], bias)

        ident = held.tile([N, N], BF16)
        make_identity(nc, ident[:])
        ones = held.tile([N, N], BF16)
        nc.vector.memset(ones[:], 1.0)

        minus_a = held.tile([N, N], BF16)
        minus_deg = held.tile([N, 1], F32)
        nc.vector.scalar_tensor_tensor(
            minus_a[:], adj_sb[:], -1.0, ident[:], ALU.mult, ALU.subtract, accum_out=minus_deg[:]
        )

        halves = [slice(0, N // 2), slice(N // 2, N)]
        nbrs_rows_ps = [psum.tile([N, N // 2], F32, name="nbrs%d" % i) for i in range(2)]
        for i, half in enumerate(halves):
            nc.tensor.matmul(nbrs_rows_ps[i][:], ones[:], adj_sb[:, half], start=True, stop=True)

        dinv_rows = held.tile([N, N], F32)
        for i, half in enumerate(halves):
            nc.scalar.activation(
                dinv_rows[:, half], nbrs_rows_ps[i][:], FUNC.Abs_reciprocal_sqrt, bias=1.0
            )
        dinv_col = held.tile([N, 1], F32)
        nc.scalar.activation(dinv_col[:], minus_deg[:], FUNC.Abs_reciprocal_sqrt)

        a_dinv = held.tile([N, N], F32)
        for half in halves:
            nc.vector.tensor_tensor(a_dinv[:, half], minus_a[:, half], dinv_rows[:, half], ALU.mult)
        a_high = a_dinv[:].bitcast(BF16)[:, 1::2]
        a_low = held.tile([N, N], BF16)
        for half in halves:
            nc.vector.tensor_tensor(
                a_low[:, half], a_dinv[:, half], a_high[:, half], ALU.subtract
            )

        hT_ps = psum.tile([N, M], F32)
        for c in range(blocks):
            nc.tensor.matmul(
                hT_ps[:], x_sb[:, c, :], w_blocks[c][:], start=(c == 0), stop=(c == blocks - 1)
            )
        gT = held.tile([N, M], BF16)
        nc.scalar.activation(gT[:], hT_ps[:], FUNC.Copy, scale=dinv_col[:, 0:1])

        quarters = [slice(q * N // 4, (q + 1) * N // 4) for q in range(4)]
        agg_ps = [psum.tile([M, N // 4], F32, name="agg%d" % i) for i in range(4)]
        for i, quarter in enumerate(quarters):
            nc.tensor.matmul(agg_ps[i][:], gT[:], a_high[:, quarter], start=True, stop=False)
            nc.tensor.matmul(agg_ps[i][:], gT[:], a_low[:, quarter], start=False, stop=True)

        v = held.tile([M, N], F32)
        slope = held.tile([M, N], F32)
        for i, quarter in enumerate(quarters):
            nc.vector.tensor_scalar(
                v[:, quarter], agg_ps[i][:], -1.0, bias_sb[:, 0:1], ALU.mult, ALU.add
            )
            nc.vector.tensor_scalar(
                slope[:, quarter], agg_ps[i][:], bias_sb[:, 0:1], SLOPE, ALU.is_lt, ALU.max
            )

        nc.vector.tensor_tensor(window[:].indirect(offsets[:]), v[:], slope[:], ALU.mult)
        nc.sync.dma_start(out, window[:])
